import numpy as np
import ml_dtypes


def mxq(x, axis, fmt="e4m3"):
    dtype, down = {"e4m3": (ml_dtypes.float8_e4m3fn, 7), "e5m2": (ml_dtypes.float8_e5m2, 14)}[fmt]
    v = np.moveaxis(np.asarray(x, np.float32).astype(ml_dtypes.bfloat16).astype(np.float64), axis, -1)
    blocks = v.reshape(v.shape[:-1] + (-1, 32))
    amax = np.abs(blocks).max(-1, keepdims=True)
    byte = np.maximum(np.where(amax > 0, np.frexp(amax)[1] - 1 + 127, 0) - down, 1)
    scale = np.exp2(byte - 127.0)
    codes = (blocks / scale).astype(np.float32).astype(dtype).astype(np.float64)
    return np.moveaxis((codes * scale).reshape(v.shape), -1, axis)


WIDE = False


def mx_kscale(k):
    if not WIDE:
        return np.ones(k)
    levels = np.array([10, -10, 5, -5, 0])
    a = np.random.permutation(np.resize(levels, k // 512 * 4)).reshape(k // 512, 4)
    idx = np.arange(k)
    return np.exp2(a[idx // 512, idx % 128 // 32])


BF16 = ml_dtypes.bfloat16


def bf(x):
    return np.asarray(x, np.float32).astype(BF16)


def f64(x):
    return np.asarray(x).astype(np.float64)


B, C, H, W, O, HS, WS, K = 1, 8192, 32, 32, 8, 4, 4, 3
PAD = 0
NI, NJ = H // HS, W // WS


def setup_inputs():
    s = mx_kscale(C)
    fan_in = C * K * K
    return {"x": bf(np.random.standard_normal((B, C, H, W)) * s[None, :, None, None]),
            "weight": bf(np.random.standard_normal((HS, WS, O, C, K, K)) / np.sqrt(fan_in) / s[None, None, None, :, None, None]),
            "bias": bf(np.random.standard_normal((HS, WS, O)) * 0.5)}


def reference(x, weight, bias):
    x, weight = f64(x), f64(weight)
    xs = x.reshape(B, C, NI, HS, NJ, WS).transpose(3, 5, 0, 2, 4, 1).reshape(HS, WS, B * NI * NJ, C)
    ws = np.stack([np.roll(weight[:, :, :, :, u, v], (u, v), (0, 1)) for u in range(K) for v in range(K)], axis=2)
    ws = ws.transpose(0, 1, 4, 2, 3).reshape(HS, WS, C, K * K * O)
    z = mxq(xs, 3, "e4m3") @ mxq(ws, 2, "e4m3")
    zi = z.reshape(HS, WS, B, NI, NJ, K, K, O).transpose(2, 3, 0, 4, 1, 5, 6, 7).reshape(B, H, W, K, K, O)
    zp = np.pad(zi, ((0, 0), (0, WS - 2 + PAD), (0, HS - 2 + PAD), (0, 0), (0, 0), (0, 0)))
    out = sum(zp[:, u:u + H, v:v + W, u, v, :] for u in range(K) for v in range(K))
    out = out.transpose(0, 3, 1, 2).reshape(B, O, NI, HS, NJ, WS)
    out = out + f64(bias).transpose(2, 0, 1)[None, :, None, :, None, :]
    return out.reshape(B, O, H, W)

@@ -1,0 +1,205 @@
+from contextlib import ExitStack
+
+import concourse.mybir as mybir
+from concourse.masks import make_identity
+
+F32 = mybir.dt.float32
+BF16 = mybir.dt.bfloat16
+U32 = mybir.dt.uint32
+U8 = mybir.dt.uint8
+FP8X4 = mybir.dt.float8_e4m3fn_x4
+ADD = mybir.AluOpType.add
+
+P = 128
+C = 8192
+K_PASS = 512
+PASSES = C // K_PASS
+PIX = 1024
+PAT = 4
+BLK = 8
+CLASSES = PAT * PAT
+O = 8
+KS = 3
+TAPS = KS * KS
+CLS_COLS = TAPS * O
+W_COLS = CLASSES * CLS_COLS
+PAIRS = CLASSES // 2
+N_MOVE = 256
+PASSES_PER_ROUND = 4
+VECTOR_TAPS = 3
+
+FLOPS = 2 * PIX * CLS_COLS * C
+
+
+def tile_patternconv_k_kernel(tc, x, weight, bias, out):
+    nc = tc.nc
+    x_view = x.rearrange("b (g u k e) y z -> g k u (b e y z)", g=PASSES, u=2, k=P, e=2)
+    w_view = weight.rearrange("h w o (g c) u v -> g (h w o) (c u v)", g=PASSES)
+    out_view = out.rearrange("b o (i h) z -> h (b o) i z", h=PAT)
+
+    with ExitStack() as ctx:
+        const = ctx.enter_context(tc.tile_pool(name="const", bufs=1))
+        loads = ctx.enter_context(tc.tile_pool(name="loads", bufs=3))
+        stage = ctx.enter_context(tc.tile_pool(name="stage", bufs=2))
+        codes = ctx.enter_context(tc.tile_pool(name="codes", bufs=2 * PASSES_PER_ROUND))
+        flip_psum = ctx.enter_context(tc.psum_pool(name="flip_psum", bufs=4))
+        z_psum = ctx.enter_context(tc.psum_pool(name="z_psum", bufs=3))
+        end_psum = ctx.enter_context(tc.psum_pool(name="end_psum", bufs=1))
+
+        ident = const.tile([P, P], F32)
+        make_identity(nc, ident[:])
+        twice = const.tile([P, 2 * PAT, 2 * PAT, O], F32)
+        ident_hwo = ident[:].rearrange("k (h w o) -> k h w o", h=PAT, w=PAT)
+        for a in range(2):
+            for b in range(2):
+                nc.vector.tensor_copy(
+                    out=twice[:, PAT * a : PAT * (a + 1), PAT * b : PAT * (b + 1), :], in_=ident_hwo
+                )
+        perm = const.tile([P, TAPS, P], F32)
+        for u in range(KS):
+            for v in range(KS):
+                nc.vector.tensor_copy(
+                    out=perm[:, KS * u + v, :].rearrange("k (p q o) -> k p q o", p=PAT, q=PAT),
+                    in_=twice[:, PAT - u : 2 * PAT - u, PAT - v : 2 * PAT - v, :],
+                )
+        block_of = const.tile([P, BLK + 1, BLK + 1], F32)
+        nc.vector.memset(block_of[:], 0.0)
+        nc.vector.tensor_tensor(
+            out=block_of[:, 0:BLK, 0:BLK],
+            in0=ident[:, 0:64].rearrange("k (i j) -> k i j", i=BLK),
+            in1=ident[:, 64:128].rearrange("k (i j) -> k i j", i=BLK),
+            op=ADD,
+        )
+        shift = const.tile([P, 4, BLK * BLK], F32)
+        for di in range(2):
+            for dj in range(2):
+                nc.vector.tensor_copy(
+                    out=shift[:, 2 * di + dj, :].rearrange("k (i j) -> k i j", i=BLK),
+                    in_=block_of[:, di : di + BLK, dj : dj + BLK],
+                )
+        LEAD = 2 * O
+        patch = const.tile([P, 512], F32)
+        nc.vector.memset(patch[:], 0.0)
+        patch_abo = patch[:, LEAD : LEAD + 6 * 8 * O].rearrange("k (b a o) -> k a b o", b=6, a=8)
+        bias_rows = const.tile([64, CLASSES * O], BF16)
+        nc.scalar.dma_start(out=bias_rows[:], in_=bias.rearrange("h w o -> (h w o)").partition_broadcast(64))
+        nc.vector.tensor_copy(
+            out=patch_abo[0:64, 2 : 2 + PAT, 2 : 2 + PAT, :],
+            in_=bias_rows[:].rearrange("k (h w o) -> k h w o", h=PAT, w=PAT),
+        )
+
+        round_codes = []
+        for g in range(PASSES):
+            w_nat = loads.tile([P, K_PASS * TAPS], BF16)
+            nc.sync.dma_start(out=w_nat[:], in_=w_view[g])
+            x_raw = loads.tile([P, 4, PIX], BF16)
+            nc.sync.dma_start(out=x_raw[:].rearrange("k (u e) n -> k u (e n)", u=2), in_=x_view[g])
+
+            w_tap = stage.tile([P, TAPS, K_PASS], BF16, align_bytes=64)
+            w_nat_tc = w_nat[:].rearrange("k (c t) -> k t c", t=TAPS)
+            nc.vector.tensor_copy(out=w_tap[:, 0:VECTOR_TAPS, :], in_=w_nat_tc[:, 0:VECTOR_TAPS, :])
+            nc.scalar.copy(out=w_tap[:, VECTOR_TAPS:TAPS, :], in_=w_nat_tc[:, VECTOR_TAPS:TAPS, :])
+            w_tap_words = w_tap[:].bitcast(F32)
+
+            w_grp = stage.tile([P, W_COLS * 4], BF16, align_bytes=64)
+            w_grp_words = w_grp[:].bitcast(F32).rearrange(
+                "k (c t o u) -> k t c o u", c=CLASSES, t=TAPS, o=O, u=2
+            )
+            for tap0 in range(0, TAPS, 2):
+                flipped = flip_psum.tile([P, 2, 2, P], F32)
+                taps_here = range(tap0, min(tap0 + 2, TAPS))
+                for tap in taps_here:
+                    for u2 in range(2):
+                        nc.tensor.transpose(
+                            flipped[:, tap - tap0, u2, :],
+                            w_tap_words[:, tap, P * u2 : P * (u2 + 1)],
+                            perm[:, tap, :],
+                        )
+                for tap in taps_here:
+                    nc.scalar.copy(
+                        out=w_grp_words[:, TAPS - 1 - tap],
+                        in_=flipped[:, tap - tap0, :, :].rearrange("k u (c o) -> k c o u", c=CLASSES),
+                    )
+
+            x_grp = stage.tile([P, PIX, 4], BF16, align_bytes=64)
+            x_raw_sorted = x_raw[:].rearrange(
+                "k t (i p j q) -> k p q i j t", i=BLK, p=PAT, j=BLK, q=PAT
+            )
+            for p in range(PAT):
+                nc.vector.tensor_copy(
+                    out=x_grp[:, 256 * p : 256 * (p + 1), :].rearrange(
+                        "k (q i j) t -> k q i j t", q=PAT, i=BLK
+                    ),
+                    in_=x_raw_sorted[:, p],
+                )
+
+            x_codes = codes.tile([P, PIX], U32, align_bytes=64)
+            x_scales = codes.tile([P, PIX], U8, align_bytes=64)
+            nc.vector.quantize_mx(
+                out=x_codes[:].bitcast(FP8X4),
+                scales=x_scales[:],
+                in_=x_grp[:].rearrange("k c t -> k (c t)"),
+            )
+            w_codes = codes.tile([P, W_COLS], U32, align_bytes=64)
+            w_scales = codes.tile([P, W_COLS], U8, align_bytes=64)
+            for c0, c1 in ((0, 1024), (1024, W_COLS)):
+                nc.vector.quantize_mx(
+                    out=w_codes[:, c0:c1].bitcast(FP8X4),
+                    scales=w_scales[:, c0:c1],
+                    in_=w_grp[:, 4 * c0 : 4 * c1],
+                )
+            round_codes.append((x_codes, x_scales, w_codes, w_scales))
+
+            if len(round_codes) < PASSES_PER_ROUND:
+                continue
+            for pair in range(PAIRS):
+                first = CLS_COLS * 2 * pair
+                window = min(first // 64 * 64, W_COLS - N_MOVE)
+                z = z_psum.tile([P, N_MOVE], F32)
+                for r, (xc, xs, wc, ws) in enumerate(round_codes):
+                    nc.tensor.matmul_mx(
+                        out=z[:],
+                        lhsT=xc[:, P * pair : P * (pair + 1)].bitcast(FP8X4),
+                        lhsT_scale=xs[:, P * pair : P * (pair + 1)],
+                        rhs=wc[:, window : window + N_MOVE].bitcast(FP8X4),
+                        rhs_scale=ws[:, window : window + N_MOVE],
+                        start=(r == 0),
+                        stop=(r == PASSES_PER_ROUND - 1),
+                    )
+                for half in range(2):
+                    cls = 2 * pair + half
+                    p, q = cls // PAT, cls % PAT
+                    rows = slice(64 * half, 64 * (half + 1))
+                    mine = first - window + CLS_COLS * half
+                    cell = patch_abo[rows, p : p + KS, q : q + KS, :]
+                    nc.vector.tensor_tensor(
+                        out=cell,
+                        in0=z[rows, mine : mine + CLS_COLS].rearrange("k (a b o) -> k a b o", a=KS, b=KS),
+                        in1=cell,
+                        op=ADD,
+                    )
+            round_codes = []
+
+        total = end_psum.tile([P, PAT, BLK * BLK], F32)
+        for w in range(PAT):
+            terms = [(di, dj) for dj in range(2 if w >= 2 else 1) for di in range(2)]
+            for n, (di, dj) in enumerate(terms):
+                b = w + 2 - PAT * dj
+                col = LEAD + 8 * O * b + (2 * O if di == 0 else -2 * O)
+                nc.tensor.matmul(
+                    total[:, w, :],
+                    lhsT=patch[:, col : col + P],
+                    rhs=shift[:, 2 * di + dj, :],
+                    start=(n == 0),
+                    stop=(n == len(terms) - 1),
+                )
+        result = const.tile([PAT * O, BLK * BLK * PAT], F32)
+        nc.vector.tensor_copy(
+            out=result[:].rearrange("k (n w) -> k n w", w=PAT),
+            in_=total[0 : PAT * O, :, :].rearrange("k w n -> k n w"),
+        )
+        for h in range(PAT):
+            nc.sync.dma_start(
+                out=out_view[h],
+                in_=result[O * h : O * (h + 1), :].rearrange("k (i z) -> k i z", i=BLK),
+            )

@@ -26,7 +26,6 @@ W_COLS = CLASSES * CLS_COLS
 PAIRS = CLASSES // 2
 N_MOVE = 256
 PASSES_PER_ROUND = 4
-VECTOR_TAPS = 3
 
 FLOPS = 2 * PIX * CLS_COLS * C
 
@@ -96,9 +95,11 @@ def tile_patternconv_k_kernel(tc, x, weight, bias, out):
             nc.sync.dma_start(out=x_raw[:].rearrange("k (u e) n -> k u (e n)", u=2), in_=x_view[g])
 
             w_tap = stage.tile([P, TAPS, K_PASS], BF16, align_bytes=64)
-            w_nat_tc = w_nat[:].rearrange("k (c t) -> k t c", t=TAPS)
-            nc.vector.tensor_copy(out=w_tap[:, 0:VECTOR_TAPS, :], in_=w_nat_tc[:, 0:VECTOR_TAPS, :])
-            nc.scalar.copy(out=w_tap[:, VECTOR_TAPS:TAPS, :], in_=w_nat_tc[:, VECTOR_TAPS:TAPS, :])
+            w_nat_ct = w_nat[:].rearrange("k (c t) -> k c t", t=TAPS)
+            w_tap_ct = w_tap[:].rearrange("k t c -> k c t")
+            nc.vector.tensor_copy(out=w_tap_ct[:, :, 0:3], in_=w_nat_ct[:, :, 0:3])
+            nc.scalar.copy(out=w_tap_ct[:, :, 3:6], in_=w_nat_ct[:, :, 3:6])
+            nc.scalar.copy(out=w_tap_ct[:, :, 6:9], in_=w_nat_ct[:, :, 6:9])
             w_tap_words = w_tap[:].bitcast(F32)
 
             w_grp = stage.tile([P, W_COLS * 4], BF16, align_bytes=64)

@@ -124,12 +124,12 @@ def tile_patternconv_k_kernel(tc, x, weight, bias, out):
 
             x_grp = stage.tile([P, PIX, 4], BF16, align_bytes=64)
             x_raw_sorted = x_raw[:].rearrange(
-                "k t (i p j q) -> k p q i j t", i=BLK, p=PAT, j=BLK, q=PAT
+                "k t (i p j q) -> k p i j t q", i=BLK, p=PAT, j=BLK, q=PAT
             )
             for p in range(PAT):
                 nc.vector.tensor_copy(
                     out=x_grp[:, 256 * p : 256 * (p + 1), :].rearrange(
-                        "k (q i j) t -> k q i j t", q=PAT, i=BLK
+                        "k (q i j) t -> k i j t q", q=PAT, i=BLK
                     ),
                     in_=x_raw_sorted[:, p],
                 )

@@ -25,9 +25,14 @@ CLS_COLS = TAPS * O
 W_COLS = CLASSES * CLS_COLS
 PAIRS = CLASSES // 2
 N_MOVE = 256
-PASSES_PER_ROUND = 4
+
+LEAD = 2 * O
 
 FLOPS = 2 * PIX * CLS_COLS * C
+
+
+def window_of(pair):
+    return min(2 * CLS_COLS * pair // 64 * 64, W_COLS - N_MOVE)
 
 
 def tile_patternconv_k_kernel(tc, x, weight, bias, out):
@@ -40,10 +45,9 @@ def tile_patternconv_k_kernel(tc, x, weight, bias, out):
         const = ctx.enter_context(tc.tile_pool(name="const", bufs=1))
         loads = ctx.enter_context(tc.tile_pool(name="loads", bufs=3))
         stage = ctx.enter_context(tc.tile_pool(name="stage", bufs=2))
-        codes = ctx.enter_context(tc.tile_pool(name="codes", bufs=2 * PASSES_PER_ROUND))
+        codes = ctx.enter_context(tc.tile_pool(name="codes", bufs=3))
         flip_psum = ctx.enter_context(tc.psum_pool(name="flip_psum", bufs=4))
-        z_psum = ctx.enter_context(tc.psum_pool(name="z_psum", bufs=3))
-        end_psum = ctx.enter_context(tc.psum_pool(name="end_psum", bufs=1))
+        z_psum = ctx.enter_context(tc.psum_pool(name="z_psum", bufs=1))
 
         ident = const.tile([P, P], F32)
         make_identity(nc, ident[:])
@@ -76,7 +80,6 @@ def tile_patternconv_k_kernel(tc, x, weight, bias, out):
                     out=shift[:, 2 * di + dj, :].rearrange("k (i j) -> k i j", i=BLK),
                     in_=block_of[:, di : di + BLK, dj : dj + BLK],
                 )
-        LEAD = 2 * O
         patch = const.tile([P, 512], F32)
         nc.vector.memset(patch[:], 0.0)
         patch_abo = patch[:, LEAD : LEAD + 6 * 8 * O].rearrange("k (b a o) -> k a b o", b=6, a=8)
@@ -87,27 +90,48 @@ def tile_patternconv_k_kernel(tc, x, weight, bias, out):
             in_=bias_rows[:].rearrange("k (h w o) -> k h w o", h=PAT, w=PAT),
         )
 
-        round_codes = []
-        for g in range(PASSES):
+        z_banks = [z_psum.tile([P, 2, N_MOVE], F32, name="z_bank%d" % b) for b in range(PAIRS // 2)]
+        held = {}
+
+        def load(g):
             w_nat = loads.tile([P, K_PASS * TAPS], BF16)
             nc.sync.dma_start(out=w_nat[:], in_=w_view[g])
             x_raw = loads.tile([P, 4, PIX], BF16)
             nc.sync.dma_start(out=x_raw[:].rearrange("k (u e) n -> k u (e n)", u=2), in_=x_view[g])
+            held["w_nat", g] = w_nat
+            held["x_raw", g] = x_raw
 
+        def sort_taps(g):
             w_tap = stage.tile([P, TAPS, K_PASS], BF16, align_bytes=64)
-            w_nat_ct = w_nat[:].rearrange("k (c t) -> k c t", t=TAPS)
+            w_nat_ct = held["w_nat", g][:].rearrange("k (c t) -> k c t", t=TAPS)
             w_tap_ct = w_tap[:].rearrange("k t c -> k c t")
             nc.vector.tensor_copy(out=w_tap_ct[:, :, 0:3], in_=w_nat_ct[:, :, 0:3])
             nc.scalar.copy(out=w_tap_ct[:, :, 3:6], in_=w_nat_ct[:, :, 3:6])
             nc.scalar.copy(out=w_tap_ct[:, :, 6:9], in_=w_nat_ct[:, :, 6:9])
-            w_tap_words = w_tap[:].bitcast(F32)
+            held["w_tap", g] = w_tap
 
+        def group_x(g):
+            x_grp = stage.tile([P, PIX, 4], BF16, align_bytes=64)
+            x_raw_sorted = held["x_raw", g][:].rearrange(
+                "k t (i p j q) -> k p i j t q", i=BLK, p=PAT, j=BLK, q=PAT
+            )
+            for p in range(PAT):
+                nc.vector.tensor_copy(
+                    out=x_grp[:, 256 * p : 256 * (p + 1), :].rearrange(
+                        "k (q i j) t -> k i j t q", q=PAT, i=BLK
+                    ),
+                    in_=x_raw_sorted[:, p],
+                )
+            held["x_grp", g] = x_grp
+
+        def flip(g):
+            w_tap_words = held["w_tap", g][:].bitcast(F32)
             w_grp = stage.tile([P, W_COLS * 4], BF16, align_bytes=64)
             w_grp_words = w_grp[:].bitcast(F32).rearrange(
                 "k (c t o u) -> k t c o u", c=CLASSES, t=TAPS, o=O, u=2
             )
             for tap0 in range(0, TAPS, 2):
-                flipped = flip_psum.tile([P, 2, 2, P], F32)
+                flipped = flip_psum.tile([P, 2, 2, P], F32, tag="flipped")
                 taps_here = range(tap0, min(tap0 + 2, TAPS))
                 for tap in taps_here:
                     for u2 in range(2):
@@ -121,26 +145,20 @@ def tile_patternconv_k_kernel(tc, x, weight, bias, out):
                         out=w_grp_words[:, TAPS - 1 - tap],
                         in_=flipped[:, tap - tap0, :, :].rearrange("k u (c o) -> k c o u", c=CLASSES),
                     )
+            held["w_grp", g] = w_grp
 
-            x_grp = stage.tile([P, PIX, 4], BF16, align_bytes=64)
-            x_raw_sorted = x_raw[:].rearrange(
-                "k t (i p j q) -> k p i j t q", i=BLK, p=PAT, j=BLK, q=PAT
-            )
-            for p in range(PAT):
-                nc.vector.tensor_copy(
-                    out=x_grp[:, 256 * p : 256 * (p + 1), :].rearrange(
-                        "k (q i j) t -> k i j t q", q=PAT, i=BLK
-                    ),
-                    in_=x_raw_sorted[:, p],
-                )
-
+        def quantise_x(g):
             x_codes = codes.tile([P, PIX], U32, align_bytes=64)
             x_scales = codes.tile([P, PIX], U8, align_bytes=64)
             nc.vector.quantize_mx(
                 out=x_codes[:].bitcast(FP8X4),
                 scales=x_scales[:],
-                in_=x_grp[:].rearrange("k c t -> k (c t)"),
+                in_=held["x_grp", g][:].rearrange("k c t -> k (c t)"),
             )
+            held["x_mx", g] = (x_codes, x_scales)
+
+        def quantise_w(g):
+            w_grp = held["w_grp", g]
             w_codes = codes.tile([P, W_COLS], U32, align_bytes=64)
             w_scales = codes.tile([P, W_COLS], U8, align_bytes=64)
             for c0, c1 in ((0, 1024), (1024, W_COLS)):
@@ -149,39 +167,53 @@ def tile_patternconv_k_kernel(tc, x, weight, bias, out):
                     scales=w_scales[:, c0:c1],
                     in_=w_grp[:, 4 * c0 : 4 * c1],
                 )
-            round_codes.append((x_codes, x_scales, w_codes, w_scales))
+            held["w_mx", g] = (w_codes, w_scales)
 
-            if len(round_codes) < PASSES_PER_ROUND:
-                continue
+        def multiply(g):
+            x_codes, x_scales = held["x_mx", g]
+            w_codes, w_scales = held["w_mx", g]
             for pair in range(PAIRS):
-                first = CLS_COLS * 2 * pair
-                window = min(first // 64 * 64, W_COLS - N_MOVE)
-                z = z_psum.tile([P, N_MOVE], F32)
-                for r, (xc, xs, wc, ws) in enumerate(round_codes):
-                    nc.tensor.matmul_mx(
-                        out=z[:],
-                        lhsT=xc[:, P * pair : P * (pair + 1)].bitcast(FP8X4),
-                        lhsT_scale=xs[:, P * pair : P * (pair + 1)],
-                        rhs=wc[:, window : window + N_MOVE].bitcast(FP8X4),
-                        rhs_scale=ws[:, window : window + N_MOVE],
-                        start=(r == 0),
-                        stop=(r == PASSES_PER_ROUND - 1),
-                    )
-                for half in range(2):
-                    cls = 2 * pair + half
-                    p, q = cls // PAT, cls % PAT
-                    rows = slice(64 * half, 64 * (half + 1))
-                    mine = first - window + CLS_COLS * half
-                    cell = patch_abo[rows, p : p + KS, q : q + KS, :]
-                    nc.vector.tensor_tensor(
-                        out=cell,
-                        in0=z[rows, mine : mine + CLS_COLS].rearrange("k (a b o) -> k a b o", a=KS, b=KS),
-                        in1=cell,
-                        op=ADD,
-                    )
-            round_codes = []
+                window = window_of(pair)
+                nc.tensor.matmul_mx(
+                    out=z_banks[pair // 2][:, pair % 2, :],
+                    lhsT=x_codes[:, P * pair : P * (pair + 1)].bitcast(FP8X4),
+                    lhsT_scale=x_scales[:, P * pair : P * (pair + 1)],
+                    rhs=w_codes[:, window : window + N_MOVE].bitcast(FP8X4),
+                    rhs_scale=w_scales[:, window : window + N_MOVE],
+                    start=(g == 0 and pair % 2 == 0),
+                    stop=(g == PASSES - 1 and pair % 2 == 1),
+                )
 
-        total = end_psum.tile([P, PAT, BLK * BLK], F32)
+        for step in range(PASSES + 3):
+            if step < PASSES:
+                load(step)
+            if 0 <= step - 1 < PASSES:
+                sort_taps(step - 1)
+                group_x(step - 1)
+            if 0 <= step - 2 < PASSES:
+                flip(step - 2)
+                quantise_x(step - 2)
+            if 0 <= step - 3 < PASSES:
+                quantise_w(step - 3)
+                multiply(step - 3)
+
+        for pair in range(PAIRS):
+            for half in range(2):
+                cls = 2 * pair + half
+                p, q = cls // PAT, cls % PAT
+                rows = slice(64 * half, 64 * (half + 1))
+                mine = CLS_COLS * cls - window_of(pair)
+                cell = patch_abo[rows, p : p + KS, q : q + KS, :]
+                nc.vector.tensor_tensor(
+                    out=cell,
+                    in0=z_banks[pair // 2][rows, pair % 2, mine : mine + CLS_COLS].rearrange(
+                        "k (a b o) -> k a b o", a=KS, b=KS
+                    ),
+                    in1=cell,
+                    op=ADD,
+                )
+
+        total = flip_psum.tile([P, PAT, BLK * BLK], F32, tag="flipped")
         for w in range(PAT):
             terms = [(di, dj) for dj in range(2 if w >= 2 else 1) for di in range(2)]
             for n, (di, dj) in enumerate(terms):

@@ -184,6 +184,7 @@ def tile_patternconv_k_kernel(tc, x, weight, bias, out):
                     stop=(g == PASSES - 1 and pair % 2 == 1),
                 )
 
+        ctx.enter_context(tc.manual_schedule())
         for step in range(PASSES + 3):
             if step < PASSES:
                 load(step)

@@ -27,6 +27,7 @@ PAIRS = CLASSES // 2
 N_MOVE = 256
 
 LEAD = 2 * O
+VECTOR_CHANNELS = 128
 
 FLOPS = 2 * PIX * CLS_COLS * C
 
@@ -105,9 +106,11 @@ def tile_patternconv_k_kernel(tc, x, weight, bias, out):
             w_tap = stage.tile([P, TAPS, K_PASS], BF16, align_bytes=64)
             w_nat_ct = held["w_nat", g][:].rearrange("k (c t) -> k c t", t=TAPS)
             w_tap_ct = w_tap[:].rearrange("k t c -> k c t")
+            cut = VECTOR_CHANNELS
             nc.vector.tensor_copy(out=w_tap_ct[:, :, 0:3], in_=w_nat_ct[:, :, 0:3])
+            nc.vector.tensor_copy(out=w_tap_ct[:, 0:cut, 6:9], in_=w_nat_ct[:, 0:cut, 6:9])
             nc.scalar.copy(out=w_tap_ct[:, :, 3:6], in_=w_nat_ct[:, :, 3:6])
-            nc.scalar.copy(out=w_tap_ct[:, :, 6:9], in_=w_nat_ct[:, :, 6:9])
+            nc.scalar.copy(out=w_tap_ct[:, cut:K_PASS, 6:9], in_=w_nat_ct[:, cut:K_PASS, 6:9])
             held["w_tap", g] = w_tap
 
         def group_x(g):
@@ -128,23 +131,23 @@ def tile_patternconv_k_kernel(tc, x, weight, bias, out):
             w_tap_words = held["w_tap", g][:].bitcast(F32)
             w_grp = stage.tile([P, W_COLS * 4], BF16, align_bytes=64)
             w_grp_words = w_grp[:].bitcast(F32).rearrange(
-                "k (c t o u) -> k t c o u", c=CLASSES, t=TAPS, o=O, u=2
+                "k (c t o u) -> k c t o u", c=CLASSES, t=TAPS, o=O, u=2
             )
-            for tap0 in range(0, TAPS, 2):
-                flipped = flip_psum.tile([P, 2, 2, P], F32, tag="flipped")
-                taps_here = range(tap0, min(tap0 + 2, TAPS))
-                for tap in taps_here:
+            for t0 in range(0, TAPS, 2):
+                here = min(2, TAPS - t0)
+                flipped = flip_psum.tile([P, 2, CLASSES, 2, O], F32, tag="flipped")
+                for t in range(here):
+                    tap = TAPS - 1 - (t0 + t)
                     for u2 in range(2):
                         nc.tensor.transpose(
-                            flipped[:, tap - tap0, u2, :],
+                            flipped[:, u2, :, t, :],
                             w_tap_words[:, tap, P * u2 : P * (u2 + 1)],
                             perm[:, tap, :],
                         )
-                for tap in taps_here:
-                    nc.scalar.copy(
-                        out=w_grp_words[:, TAPS - 1 - tap],
-                        in_=flipped[:, tap - tap0, :, :].rearrange("k u (c o) -> k c o u", c=CLASSES),
-                    )
+                nc.scalar.copy(
+                    out=w_grp_words[:, :, t0 : t0 + here, :, :],
+                    in_=flipped[:, :, :, 0:here, :].rearrange("k u c t o -> k c t o u"),
+                )
             held["w_grp", g] = w_grp
 
         def quantise_x(g):

from contextlib import ExitStack

import concourse.mybir as mybir
from concourse.masks import make_identity

F32 = mybir.dt.float32
BF16 = mybir.dt.bfloat16
U32 = mybir.dt.uint32
U8 = mybir.dt.uint8
FP8X4 = mybir.dt.float8_e4m3fn_x4
ADD = mybir.AluOpType.add

P = 128
C = 8192
K_PASS = 512
PASSES = C // K_PASS
PIX = 1024
PAT = 4
BLK = 8
CLASSES = PAT * PAT
O = 8
KS = 3
TAPS = KS * KS
CLS_COLS = TAPS * O
W_COLS = CLASSES * CLS_COLS
PAIRS = CLASSES // 2
N_MOVE = 256

LEAD = 2 * O
VECTOR_CHANNELS = 128

FLOPS = 2 * PIX * CLS_COLS * C


def window_of(pair):
    return min(2 * CLS_COLS * pair // 64 * 64, W_COLS - N_MOVE)


def tile_patternconv_k_kernel(tc, x, weight, bias, out):
    nc = tc.nc
    x_view = x.rearrange("b (g u k e) y z -> g k u (b e y z)", g=PASSES, u=2, k=P, e=2)
    w_view = weight.rearrange("h w o (g c) u v -> g (h w o) (c u v)", g=PASSES)
    out_view = out.rearrange("b o (i h) z -> h (b o) i z", h=PAT)

    with ExitStack() as ctx:
        const = ctx.enter_context(tc.tile_pool(name="const", bufs=1))
        loads = ctx.enter_context(tc.tile_pool(name="loads", bufs=3))
        stage = ctx.enter_context(tc.tile_pool(name="stage", bufs=2))
        codes = ctx.enter_context(tc.tile_pool(name="codes", bufs=3))
        flip_psum = ctx.enter_context(tc.psum_pool(name="flip_psum", bufs=4))
        z_psum = ctx.enter_context(tc.psum_pool(name="z_psum", bufs=1))

        ident = const.tile([P, P], F32)
        make_identity(nc, ident[:])
        twice = const.tile([P, 2 * PAT, 2 * PAT, O], F32)
        ident_hwo = ident[:].rearrange("k (h w o) -> k h w o", h=PAT, w=PAT)
        for a in range(2):
            for b in range(2):
                nc.vector.tensor_copy(
                    out=twice[:, PAT * a : PAT * (a + 1), PAT * b : PAT * (b + 1), :], in_=ident_hwo
                )
        perm = const.tile([P, TAPS, P], F32)
        for u in range(KS):
            for v in range(KS):
                nc.vector.tensor_copy(
                    out=perm[:, KS * u + v, :].rearrange("k (p q o) -> k p q o", p=PAT, q=PAT),
                    in_=twice[:, PAT - u : 2 * PAT - u, PAT - v : 2 * PAT - v, :],
                )
        block_of = const.tile([P, BLK + 1, BLK + 1], F32)
        nc.vector.memset(block_of[:], 0.0)
        nc.vector.tensor_tensor(
            out=block_of[:, 0:BLK, 0:BLK],
            in0=ident[:, 0:64].rearrange("k (i j) -> k i j", i=BLK),
            in1=ident[:, 64:128].rearrange("k (i j) -> k i j", i=BLK),
            op=ADD,
        )
        shift = const.tile([P, 4, BLK * BLK], F32)
        for di in range(2):
            for dj in range(2):
                nc.vector.tensor_copy(
                    out=shift[:, 2 * di + dj, :].rearrange("k (i j) -> k i j", i=BLK),
                    in_=block_of[:, di : di + BLK, dj : dj + BLK],
                )
        patch = const.tile([P, 512], F32)
        nc.vector.memset(patch[:], 0.0)
        patch_abo = patch[:, LEAD : LEAD + 6 * 8 * O].rearrange("k (b a o) -> k a b o", b=6, a=8)
        bias_rows = const.tile([64, CLASSES * O], BF16)
        nc.scalar.dma_start(out=bias_rows[:], in_=bias.rearrange("h w o -> (h w o)").partition_broadcast(64))
        nc.vector.tensor_copy(
            out=patch_abo[0:64, 2 : 2 + PAT, 2 : 2 + PAT, :],
            in_=bias_rows[:].rearrange("k (h w o) -> k h w o", h=PAT, w=PAT),
        )

        z_banks = [z_psum.tile([P, 2, N_MOVE], F32, name="z_bank%d" % b) for b in range(PAIRS // 2)]
        held = {}

        def load(g):
            w_nat = loads.tile([P, K_PASS * TAPS], BF16)
            nc.sync.dma_start(out=w_nat[:], in_=w_view[g])
            x_raw = loads.tile([P, 4, PIX], BF16)
            nc.sync.dma_start(out=x_raw[:].rearrange("k (u e) n -> k u (e n)", u=2), in_=x_view[g])
            held["w_nat", g] = w_nat
            held["x_raw", g] = x_raw

        def sort_taps(g):
            w_tap = stage.tile([P, TAPS, K_PASS], BF16, align_bytes=64)
            w_nat_ct = held["w_nat", g][:].rearrange("k (c t) -> k c t", t=TAPS)
            w_tap_ct = w_tap[:].rearrange("k t c -> k c t")
            cut = VECTOR_CHANNELS
            nc.vector.tensor_copy(out=w_tap_ct[:, :, 0:3], in_=w_nat_ct[:, :, 0:3])
            nc.vector.tensor_copy(out=w_tap_ct[:, 0:cut, 6:9], in_=w_nat_ct[:, 0:cut, 6:9])
            nc.scalar.copy(out=w_tap_ct[:, :, 3:6], in_=w_nat_ct[:, :, 3:6])
            nc.scalar.copy(out=w_tap_ct[:, cut:K_PASS, 6:9], in_=w_nat_ct[:, cut:K_PASS, 6:9])
            held["w_tap", g] = w_tap

        def group_x(g):
            x_grp = stage.tile([P, PIX, 4], BF16, align_bytes=64)
            x_raw_sorted = held["x_raw", g][:].rearrange(
                "k t (i p j q) -> k p i j t q", i=BLK, p=PAT, j=BLK, q=PAT
            )
            for p in range(PAT):
                nc.vector.tensor_copy(
                    out=x_grp[:, 256 * p : 256 * (p + 1), :].rearrange(
                        "k (q i j) t -> k i j t q", q=PAT, i=BLK
                    ),
                    in_=x_raw_sorted[:, p],
                )
            held["x_grp", g] = x_grp

        def flip(g):
            w_tap_words = held["w_tap", g][:].bitcast(F32)
            w_grp = stage.tile([P, W_COLS * 4], BF16, align_bytes=64)
            w_grp_words = w_grp[:].bitcast(F32).rearrange(
                "k (c t o u) -> k c t o u", c=CLASSES, t=TAPS, o=O, u=2
            )
            for t0 in range(0, TAPS, 2):
                here = min(2, TAPS - t0)
                flipped = flip_psum.tile([P, 2, CLASSES, 2, O], F32, tag="flipped")
                for t in range(here):
                    tap = TAPS - 1 - (t0 + t)
                    for u2 in range(2):
                        nc.tensor.transpose(
                            flipped[:, u2, :, t, :],
                            w_tap_words[:, tap, P * u2 : P * (u2 + 1)],
                            perm[:, tap, :],
                        )
                nc.scalar.copy(
                    out=w_grp_words[:, :, t0 : t0 + here, :, :],
                    in_=flipped[:, :, :, 0:here, :].rearrange("k u c t o -> k c t o u"),
                )
            held["w_grp", g] = w_grp

        def quantise_x(g):
            x_codes = codes.tile([P, PIX], U32, align_bytes=64)
            x_scales = codes.tile([P, PIX], U8, align_bytes=64)
            nc.vector.quantize_mx(
                out=x_codes[:].bitcast(FP8X4),
                scales=x_scales[:],
                in_=held["x_grp", g][:].rearrange("k c t -> k (c t)"),
            )
            held["x_mx", g] = (x_codes, x_scales)

        def quantise_w(g):
            w_grp = held["w_grp", g]
            w_codes = codes.tile([P, W_COLS], U32, align_bytes=64)
            w_scales = codes.tile([P, W_COLS], U8, align_bytes=64)
            for c0, c1 in ((0, 1024), (1024, W_COLS)):
                nc.vector.quantize_mx(
                    out=w_codes[:, c0:c1].bitcast(FP8X4),
                    scales=w_scales[:, c0:c1],
                    in_=w_grp[:, 4 * c0 : 4 * c1],
                )
            held["w_mx", g] = (w_codes, w_scales)

        def multiply(g):
            x_codes, x_scales = held["x_mx", g]
            w_codes, w_scales = held["w_mx", g]
            for pair in range(PAIRS):
                window = window_of(pair)
                nc.tensor.matmul_mx(
                    out=z_banks[pair // 2][:, pair % 2, :],
                    lhsT=x_codes[:, P * pair : P * (pair + 1)].bitcast(FP8X4),
                    lhsT_scale=x_scales[:, P * pair : P * (pair + 1)],
                    rhs=w_codes[:, window : window + N_MOVE].bitcast(FP8X4),
                    rhs_scale=w_scales[:, window : window + N_MOVE],
                    start=(g == 0 and pair % 2 == 0),
                    stop=(g == PASSES - 1 and pair % 2 == 1),
                )

        ctx.enter_context(tc.manual_schedule())
        for step in range(PASSES + 3):
            if step < PASSES:
                load(step)
            if 0 <= step - 1 < PASSES:
                sort_taps(step - 1)
                group_x(step - 1)
            if 0 <= step - 2 < PASSES:
                flip(step - 2)
                quantise_x(step - 2)
            if 0 <= step - 3 < PASSES:
                quantise_w(step - 3)
                multiply(step - 3)

        for pair in range(PAIRS):
            for half in range(2):
                cls = 2 * pair + half
                p, q = cls // PAT, cls % PAT
                rows = slice(64 * half, 64 * (half + 1))
                mine = CLS_COLS * cls - window_of(pair)
                cell = patch_abo[rows, p : p + KS, q : q + KS, :]
                nc.vector.tensor_tensor(
                    out=cell,
                    in0=z_banks[pair // 2][rows, pair % 2, mine : mine + CLS_COLS].rearrange(
                        "k (a b o) -> k a b o", a=KS, b=KS
                    ),
                    in1=cell,
                    op=ADD,
                )

        total = flip_psum.tile([P, PAT, BLK * BLK], F32, tag="flipped")
        for w in range(PAT):
            terms = [(di, dj) for dj in range(2 if w >= 2 else 1) for di in range(2)]
            for n, (di, dj) in enumerate(terms):
                b = w + 2 - PAT * dj
                col = LEAD + 8 * O * b + (2 * O if di == 0 else -2 * O)
                nc.tensor.matmul(
                    total[:, w, :],
                    lhsT=patch[:, col : col + P],
                    rhs=shift[:, 2 * di + dj, :],
                    start=(n == 0),
                    stop=(n == len(terms) - 1),
                )
        result = const.tile([PAT * O, BLK * BLK * PAT], F32)
        nc.vector.tensor_copy(
            out=result[:].rearrange("k (n w) -> k n w", w=PAT),
            in_=total[0 : PAT * O, :, :].rearrange("k w n -> k n w"),
        )
        for h in range(PAT):
            nc.sync.dma_start(
                out=out_view[h],
                in_=result[O * h : O * (h + 1), :].rearrange("k (i z) -> k i z", i=BLK),
            )
